import numpy as np
import ml_dtypes


def mxq(x, axis, fmt="e4m3"):
    dtype, down = {"e4m3": (ml_dtypes.float8_e4m3fn, 7), "e5m2": (ml_dtypes.float8_e5m2, 14)}[fmt]
    v = np.moveaxis(np.asarray(x, np.float32).astype(ml_dtypes.bfloat16).astype(np.float64), axis, -1)
    blocks = v.reshape(v.shape[:-1] + (-1, 32))
    amax = np.abs(blocks).max(-1, keepdims=True)
    byte = np.maximum(np.where(amax > 0, np.frexp(amax)[1] - 1 + 127, 0) - down, 1)
    scale = np.exp2(byte - 127.0)
    codes = (blocks / scale).astype(np.float32).astype(dtype).astype(np.float64)
    return np.moveaxis((codes * scale).reshape(v.shape), -1, axis)


WIDE = False


def mx_kscale(k):
    if not WIDE:
        return np.ones(k)
    levels = np.array([10, -10, 5, -5, 0])
    a = np.random.permutation(np.resize(levels, k // 512 * 4)).reshape(k // 512, 4)
    idx = np.arange(k)
    return np.exp2(a[idx // 512, idx % 128 // 32])


BF16 = ml_dtypes.bfloat16


def bf(x):
    return np.asarray(x, np.float32).astype(BF16)


def f64(x):
    return np.asarray(x).astype(np.float64)


B, T, D, H, E, C = 2, 1024, 1024, 8, 1024, 512
HD = D // H
EPS = 1e-5


def setup_inputs():
    s = mx_kscale(D)
    fall = 0.35 / np.sqrt(1.0 + np.arange(T))
    return {"ret": bf(np.random.standard_normal((B, T, H, HD)) * fall[None, :, None, None]),
            "gamma": bf((1.0 + 0.1 * np.random.standard_normal(D)) * s),
            "beta": bf(0.1 * np.random.standard_normal(D) * s),
            "Wo": bf(np.random.standard_normal((D, E)) / np.sqrt(D) / s[:, None]),
            "bo": bf(0.1 * np.random.standard_normal(E))}


def reference(ret, gamma, beta, Wo, bo):
    r = f64(ret)
    mu = r.mean(-1, keepdims=True)
    var = r.var(-1, keepdims=True)
    z = (r - mu) / np.sqrt(var + EPS)
    y = z.reshape(B, T, D) * f64(gamma) + f64(beta)
    return (mxq(y, 2, "e4m3") @ mxq(f64(Wo), 0, "e4m3")) + f64(bo)

@@ -1,0 +1,221 @@
+from contextlib import ExitStack
+
+import concourse.mybir as mybir
+from concourse.masks import make_identity
+
+FLOPS = 2 * 2048 * 1024 * 1024
+
+BF16 = mybir.dt.bfloat16
+F32 = mybir.dt.float32
+U32 = mybir.dt.uint32
+U8 = mybir.dt.uint8
+FP8X4 = mybir.dt.float8_e4m3fn_x4
+ALU = mybir.AluOpType
+ACT = mybir.ActivationFunctionType
+
+P = 128
+D = 1024
+E = 1024
+H = 8
+SLOTS = 16
+GS = 2
+NG = SLOTS // GS
+GT = GS * P
+EPS = 1e-5
+QLAG = 4
+
+
+def tile_retentivenetwork_pb_kernel(tc, ret, gamma, beta, Wo, bo, out):
+    nc = tc.nc
+    ret_v = ret.rearrange("b (q j) h c -> (b q) j (h c)", j=SLOTS)
+    out_v = out.rearrange("b (q j) e -> (b q) j e", j=SLOTS)
+    wo_v = Wo.rearrange("(a p) n -> p a n", p=P)
+
+    with ExitStack() as ctx:
+        const = ctx.enter_context(tc.tile_pool(name="const", bufs=1))
+        small = ctx.enter_context(tc.tile_pool(name="small", bufs=4))
+        zpool = ctx.enter_context(tc.tile_pool(name="zpool", bufs=3))
+        ypool = ctx.enter_context(tc.tile_pool(name="ypool", bufs=4))
+        cpool = ctx.enter_context(tc.tile_pool(name="cpool", bufs=3))
+        opool = ctx.enter_context(tc.tile_pool(name="opool", bufs=3))
+        tpsum = ctx.enter_context(tc.psum_pool(name="tpsum", bufs=4))
+        apsum = ctx.enter_context(tc.psum_pool(name="apsum", bufs=4))
+        ctx.enter_context(tc.manual_schedule())
+
+        xs = []
+        for g in range(NG):
+            xg = const.tile([P, GS, D], BF16, name="x%d" % g)
+            xs.append(xg)
+        wraw = const.tile([P, 8, E], BF16, name="wraw")
+
+        def load_x(g):
+            nc.sync.dma_start(out=xs[g][:], in_=ret_v[:, g * GS:(g + 1) * GS, :])
+
+        def load_w(a):
+            nc.sync.dma_start(out=wraw[:, 4 * a:4 * a + 4, :], in_=wo_v[:, 4 * a:4 * a + 4, :])
+
+        load_x(0)
+        load_x(1)
+        load_w(0)
+        load_x(2)
+        load_w(1)
+        for g in range(3, NG):
+            load_x(g)
+
+        gb = const.tile([P, P], BF16, name="gb")
+        nc.vector.memset(gb[:], 0.0)
+        one = const.tile([P, 1], F32, name="one")
+        nc.vector.memset(one[:], 1.0)
+        nc.scalar.dma_start(out=gb[0:8, :], in_=gamma.rearrange("(h c) -> h c", c=P))
+        nc.scalar.dma_start(out=gb[8:16, :], in_=beta.rearrange("(h c) -> h c", c=P))
+        bias_b = const.tile([P, E], BF16, name="bias_b")
+        nc.scalar.dma_start(out=bias_b[:], in_=bo.partition_broadcast(P))
+        warm = const.tile([P, 1], F32, name="warm")
+        nc.scalar.activation(out=warm[:], in_=one[:], func=ACT.Sqrt)
+
+        ident = const.tile([P, P], F32, name="ident")
+        make_identity(nc, ident[:])
+
+        gbf = const.tile([P, P], F32, name="gbf")
+        nc.scalar.copy(out=gbf[:], in_=gb[:])
+        gps = tpsum.tile([P, 512], F32, tag="zt", name="gps")
+        nc.tensor.transpose(out=gps[:, 0:P], in_=gbf[:], identity=ident[:])
+        gbT = const.tile([P, 16], F32, name="gbT")
+        nc.scalar.copy(out=gbT[:], in_=gps[:, 0:16])
+
+        wgrp = const.tile([P, 2, E, 4], BF16, name="wgrp", align_bytes=64)
+        wc = const.tile([P, 2, E], U32, name="wc", align_bytes=64)
+        ws = const.tile([P, 2, E], U8, name="ws", align_bytes=64)
+
+        def regroup_w(a, half):
+            cols = slice(half * 512, (half + 1) * 512)
+            nc.gpsimd.tensor_scalar(
+                out=wgrp[:, a, cols, :], in0=wraw[:, 4 * a:4 * a + 4, cols].rearrange("p t c -> p c t"),
+                scalar1=1.0, scalar2=0.0, op0=ALU.mult, op1=ALU.add,
+            )
+
+        def quantise_w(a):
+            nc.vector.quantize_mx(
+                out=wc[:, a, :].bitcast(FP8X4), scales=ws[:, a, :],
+                in_=wgrp[:, a, :, :].rearrange("p c t -> p (c t)"),
+            )
+
+        sums, wsum, rstd, nb, z, zt, yp, yg, yc, ys, acc = {}, {}, {}, {}, {}, {}, {}, {}, {}, {}, {}
+        U = GS * H
+
+        def stats_first(g):
+            st = small.tile([P, U, 6], F32, name="st")
+            for s in range(GS):
+                for h in range(H):
+                    nc.vector.bn_stats(out=st[:, s * H + h, :], in_=xs[g][:, s, h * P:(h + 1) * P])
+            sums[g] = small.tile([P, U, 3], F32, name="sums")
+            nc.vector.tensor_tensor(out=sums[g][:], in0=st[:, :, 0:3], in1=st[:, :, 3:6], op=ALU.add)
+            dif = small.tile([P, U, 1], F32, name="dif")
+            nc.vector.tensor_tensor(out=dif[:], in0=st[:, :, 1:2], in1=st[:, :, 4:5], op=ALU.subtract)
+            q32 = small.tile([P, U, 1], F32, name="q32")
+            nc.vector.scalar_tensor_tensor(out=q32[:], in0=dif[:], scalar=32.0, in1=dif[:], op0=ALU.mult, op1=ALU.mult)
+            w128 = small.tile([P, U, 1], F32, name="w128")
+            nc.vector.scalar_tensor_tensor(out=w128[:], in0=q32[:], scalar=P * EPS, in1=sums[g][:, :, 2:3], op0=ALU.add, op1=ALU.add)
+            wsum[g] = small.tile([P, U, 1], F32, name="std")
+            nc.scalar.activation(out=wsum[g][:], in_=w128[:], func=ACT.Sqrt, scale=1.0 / P)
+
+        def stats_second(g):
+            rstd[g] = small.tile([P, U, 1], F32, name="rstd")
+            nc.vector.reciprocal(out=rstd[g][:], in_=wsum[g][:])
+            nb[g] = small.tile([P, U, 1], F32, name="nb")
+            nc.vector.scalar_tensor_tensor(out=nb[g][:], in0=sums[g][:, :, 1:2], scalar=-0.5, in1=rstd[g][:], op0=ALU.mult, op1=ALU.mult)
+
+        def normalise(g, heads):
+            if heads[0] == 0:
+                z[g] = zpool.tile([P, GS, D], F32, name="z")
+            for h in heads:
+                for s in range(GS):
+                    u = s * H + h
+                    nc.scalar.activation(
+                        out=z[g][:, s, h * P:(h + 1) * P], in_=xs[g][:, s, h * P:(h + 1) * P],
+                        func=ACT.Identity, bias=nb[g][:, u, :], scale=rstd[g][:, u, :],
+                    )
+
+        def turn(g, heads):
+            for h in heads:
+                zt[(g, h)] = tpsum.tile([P, 512], F32, tag="zt", name="zt")
+                for s in range(GS):
+                    nc.tensor.transpose(out=zt[(g, h)][:, s * P:(s + 1) * P], in_=z[g][:, s, h * P:(h + 1) * P], identity=ident[:])
+
+        def leave_psum(g, heads):
+            if heads[0] == 0:
+                yp[g] = ypool.tile([P, H, GT], BF16, name="yp")
+            for h in heads:
+                nc.scalar.activation(
+                    out=yp[g][:, h, :], in_=zt[(g, h)][:, 0:GT], func=ACT.Identity,
+                    bias=gbT[:, 8 + h:9 + h], scale=gbT[:, h:h + 1],
+                )
+
+        def regroup_y(g, a):
+            if a == 0:
+                yg[g] = ypool.tile([P, 2, GT, 4], BF16, name="yg", align_bytes=64)
+            nc.gpsimd.tensor_scalar(
+                out=yg[g][:, a, :, :], in0=yp[g][:, 4 * a:4 * a + 4, :].rearrange("p t c -> p c t"),
+                scalar1=1.0, scalar2=0.0, op0=ALU.mult, op1=ALU.add,
+            )
+
+        def quantise_y(g):
+            yc[g] = cpool.tile([P, 2 * GT], U32, name="yc", align_bytes=64)
+            ys[g] = cpool.tile([P, 2 * GT], U8, name="ys", align_bytes=64)
+            nc.vector.quantize_mx(out=yc[g][:].bitcast(FP8X4), scales=ys[g][:], in_=yg[g][:].rearrange("p a c t -> p (a c t)"))
+
+        def project(g):
+            for s in range(GS):
+                for n in range(2):
+                    acc[(g, s, n)] = apsum.tile([P, 512], F32, name="acc")
+                    for a in range(2):
+                        m_cols = slice(a * GT + s * P, a * GT + (s + 1) * P)
+                        n_cols = slice(n * 512, (n + 1) * 512)
+                        nc.tensor.matmul_mx(
+                            out=acc[(g, s, n)][:],
+                            lhsT=yc[g][:, m_cols].bitcast(FP8X4), lhsT_scale=ys[g][:, m_cols],
+                            rhs=wc[:, a, n_cols].bitcast(FP8X4), rhs_scale=ws[:, a, n_cols],
+                            start=(a == 0), stop=(a == 1),
+                        )
+
+        def finish(g):
+            o = opool.tile([P, GS, E], F32, name="o")
+            for s in range(GS):
+                for n in range(2):
+                    nc.vector.tensor_tensor(out=o[:, s, n * 512:(n + 1) * 512], in0=acc[(g, s, n)][:], in1=bias_b[:, n * 512:(n + 1) * 512], op=ALU.add)
+            nc.sync.dma_start(out=out_v[:, g * GS:(g + 1) * GS, :], in_=o[:])
+
+        def live(g):
+            return 0 <= g < NG
+
+        LOW = [0, 1, 2, 3]
+        HIGH = [4, 5, 6, 7]
+        for a in range(2):
+            for half in range(2):
+                regroup_w(a, half)
+        for k in range(NG + QLAG + 2):
+            if live(k):
+                stats_first(k)
+            if live(k - 1):
+                stats_second(k - 1)
+            for a in range(2):
+                if k == 3 + a:
+                    quantise_w(a)
+            if live(k - QLAG):
+                quantise_y(k - QLAG)
+            if live(k - QLAG - 1):
+                finish(k - QLAG - 1)
+            if live(k - QLAG):
+                project(k - QLAG)
+            j = k - 1
+            if live(j):
+                normalise(j, LOW)
+            if live(j - 1):
+                leave_psum(j - 1, HIGH)
+                regroup_y(j - 1, 1)
+            if live(j):
+                turn(j, LOW)
+                normalise(j, HIGH)
+                leave_psum(j, LOW)
+                regroup_y(j, 0)
+                turn(j, HIGH)

@@ -22,7 +22,11 @@ GS = 2
 NG = SLOTS // GS
 GT = GS * P
 EPS = 1e-5
-QLAG = 4
+QLAG = 3
+R_ENG = ["S","V"]
+W_ENG = ["V","V","V","V"]
+W_AT = [1,1,2,2]
+WQ_AT = [1,2]
 
 
 def tile_retentivenetwork_pb_kernel(tc, ret, gamma, beta, Wo, bo, out):
@@ -47,6 +51,7 @@ def tile_retentivenetwork_pb_kernel(tc, ret, gamma, beta, Wo, bo, out):
             xg = const.tile([P, GS, D], BF16, name="x%d" % g)
             xs.append(xg)
         wraw = const.tile([P, 8, E], BF16, name="wraw")
+        bias_b = const.tile([P, E], BF16, name="bias_b")
 
         def load_x(g):
             nc.sync.dma_start(out=xs[g][:], in_=ret_v[:, g * GS:(g + 1) * GS, :])
@@ -54,6 +59,12 @@ def tile_retentivenetwork_pb_kernel(tc, ret, gamma, beta, Wo, bo, out):
         def load_w(a):
             nc.sync.dma_start(out=wraw[:, 4 * a:4 * a + 4, :], in_=wo_v[:, 4 * a:4 * a + 4, :])
 
+        gb = const.tile([P, P], BF16, name="gb")
+        nc.vector.memset(gb[:], 0.0)
+        one = const.tile([P, 1], F32, name="one")
+        nc.vector.memset(one[:], 1.0)
+        nc.scalar.dma_start(out=gb[0:8, :], in_=gamma.rearrange("(h c) -> h c", c=P))
+        nc.scalar.dma_start(out=gb[8:16, :], in_=beta.rearrange("(h c) -> h c", c=P))
         load_x(0)
         load_x(1)
         load_w(0)
@@ -61,38 +72,32 @@ def tile_retentivenetwork_pb_kernel(tc, ret, gamma, beta, Wo, bo, out):
         load_w(1)
         for g in range(3, NG):
             load_x(g)
-
-        gb = const.tile([P, P], BF16, name="gb")
-        nc.vector.memset(gb[:], 0.0)
-        one = const.tile([P, 1], F32, name="one")
-        nc.vector.memset(one[:], 1.0)
-        nc.scalar.dma_start(out=gb[0:8, :], in_=gamma.rearrange("(h c) -> h c", c=P))
-        nc.scalar.dma_start(out=gb[8:16, :], in_=beta.rearrange("(h c) -> h c", c=P))
-        bias_b = const.tile([P, E], BF16, name="bias_b")
-        nc.scalar.dma_start(out=bias_b[:], in_=bo.partition_broadcast(P))
+        nc.sync.dma_start(out=bias_b[:], in_=bo.partition_broadcast(P))
         warm = const.tile([P, 1], F32, name="warm")
         nc.scalar.activation(out=warm[:], in_=one[:], func=ACT.Sqrt)
 
         ident = const.tile([P, P], F32, name="ident")
         make_identity(nc, ident[:])
-
         gbf = const.tile([P, P], F32, name="gbf")
-        nc.scalar.copy(out=gbf[:], in_=gb[:])
-        gps = tpsum.tile([P, 512], F32, tag="zt", name="gps")
-        nc.tensor.transpose(out=gps[:, 0:P], in_=gbf[:], identity=ident[:])
         gbT = const.tile([P, 16], F32, name="gbT")
-        nc.scalar.copy(out=gbT[:], in_=gps[:, 0:16])
+        gps = apsum.tile([P, 512], F32, tag="acc", name="gps")
 
         wgrp = const.tile([P, 2, E, 4], BF16, name="wgrp", align_bytes=64)
         wc = const.tile([P, 2, E], U32, name="wc", align_bytes=64)
         ws = const.tile([P, 2, E], U8, name="ws", align_bytes=64)
 
-        def regroup_w(a, half):
+        def regroup(eng, dst, src):
+            if eng == "G":
+                nc.gpsimd.tensor_scalar(out=dst, in0=src.rearrange("p t c -> p c t"), scalar1=1.0, scalar2=0.0, op0=ALU.mult, op1=ALU.add)
+            elif eng == "V":
+                nc.vector.tensor_copy(out=dst.rearrange("p (c i) t -> p c t i", i=4), in_=src.rearrange("p t (c i) -> p c t i", i=4))
+            else:
+                nc.scalar.copy(out=dst.rearrange("p (c i) t -> p c t i", i=4), in_=src.rearrange("p t (c i) -> p c t i", i=4))
+
+        def regroup_w(i):
+            a, half = divmod(i, 2)
             cols = slice(half * 512, (half + 1) * 512)
-            nc.gpsimd.tensor_scalar(
-                out=wgrp[:, a, cols, :], in0=wraw[:, 4 * a:4 * a + 4, cols].rearrange("p t c -> p c t"),
-                scalar1=1.0, scalar2=0.0, op0=ALU.mult, op1=ALU.add,
-            )
+            regroup(W_ENG[i], wgrp[:, a, cols, :], wraw[:, 4 * a:4 * a + 4, cols])
 
         def quantise_w(a):
             nc.vector.quantize_mx(
@@ -100,7 +105,7 @@ def tile_retentivenetwork_pb_kernel(tc, ret, gamma, beta, Wo, bo, out):
                 in_=wgrp[:, a, :, :].rearrange("p c t -> p (c t)"),
             )
 
-        sums, wsum, rstd, nb, z, zt, yp, yg, yc, ys, acc = {}, {}, {}, {}, {}, {}, {}, {}, {}, {}, {}
+        sums, std, rstd, nb, z, zt, yp, yg, yc, ys, acc = {}, {}, {}, {}, {}, {}, {}, {}, {}, {}, {}
         U = GS * H
 
         def stats_first(g):
@@ -116,12 +121,12 @@ def tile_retentivenetwork_pb_kernel(tc, ret, gamma, beta, Wo, bo, out):
             nc.vector.scalar_tensor_tensor(out=q32[:], in0=dif[:], scalar=32.0, in1=dif[:], op0=ALU.mult, op1=ALU.mult)
             w128 = small.tile([P, U, 1], F32, name="w128")
             nc.vector.scalar_tensor_tensor(out=w128[:], in0=q32[:], scalar=P * EPS, in1=sums[g][:, :, 2:3], op0=ALU.add, op1=ALU.add)
-            wsum[g] = small.tile([P, U, 1], F32, name="std")
-            nc.scalar.activation(out=wsum[g][:], in_=w128[:], func=ACT.Sqrt, scale=1.0 / P)
+            std[g] = small.tile([P, U, 1], F32, name="std")
+            nc.scalar.activation(out=std[g][:], in_=w128[:], func=ACT.Sqrt, scale=1.0 / P)
 
         def stats_second(g):
             rstd[g] = small.tile([P, U, 1], F32, name="rstd")
-            nc.vector.reciprocal(out=rstd[g][:], in_=wsum[g][:])
+            nc.vector.reciprocal(out=rstd[g][:], in_=std[g][:])
             nb[g] = small.tile([P, U, 1], F32, name="nb")
             nc.vector.scalar_tensor_tensor(out=nb[g][:], in0=sums[g][:, :, 1:2], scalar=-0.5, in1=rstd[g][:], op0=ALU.mult, op1=ALU.mult)
 
@@ -154,10 +159,7 @@ def tile_retentivenetwork_pb_kernel(tc, ret, gamma, beta, Wo, bo, out):
         def regroup_y(g, a):
             if a == 0:
                 yg[g] = ypool.tile([P, 2, GT, 4], BF16, name="yg", align_bytes=64)
-            nc.gpsimd.tensor_scalar(
-                out=yg[g][:, a, :, :], in0=yp[g][:, 4 * a:4 * a + 4, :].rearrange("p t c -> p c t"),
-                scalar1=1.0, scalar2=0.0, op0=ALU.mult, op1=ALU.add,
-            )
+            regroup(R_ENG[a], yg[g][:, a, :, :], yp[g][:, 4 * a:4 * a + 4, :])
 
         def quantise_y(g):
             yc[g] = cpool.tile([P, 2 * GT], U32, name="yc", align_bytes=64)
@@ -167,7 +169,7 @@ def tile_retentivenetwork_pb_kernel(tc, ret, gamma, beta, Wo, bo, out):
         def project(g):
             for s in range(GS):
                 for n in range(2):
-                    acc[(g, s, n)] = apsum.tile([P, 512], F32, name="acc")
+                    acc[(g, s, n)] = apsum.tile([P, 512], F32, tag="acc", name="acc")
                     for a in range(2):
                         m_cols = slice(a * GT + s * P, a * GT + (s + 1) * P)
                         n_cols = slice(n * 512, (n + 1) * 512)
@@ -183,6 +185,7 @@ def tile_retentivenetwork_pb_kernel(tc, ret, gamma, beta, Wo, bo, out):
             for s in range(GS):
                 for n in range(2):
                     nc.vector.tensor_tensor(out=o[:, s, n * 512:(n + 1) * 512], in0=acc[(g, s, n)][:], in1=bias_b[:, n * 512:(n + 1) * 512], op=ALU.add)
+
             nc.sync.dma_start(out=out_v[:, g * GS:(g + 1) * GS, :], in_=o[:])
 
         def live(g):
@@ -190,16 +193,19 @@ def tile_retentivenetwork_pb_kernel(tc, ret, gamma, beta, Wo, bo, out):
 
         LOW = [0, 1, 2, 3]
         HIGH = [4, 5, 6, 7]
-        for a in range(2):
-            for half in range(2):
-                regroup_w(a, half)
+        for i in range(4):
+            if W_ENG[i] == "G":
+                regroup_w(i)
         for k in range(NG + QLAG + 2):
             if live(k):
                 stats_first(k)
             if live(k - 1):
                 stats_second(k - 1)
+            for i in range(4):
+                if W_ENG[i] != "G" and W_AT[i] == k:
+                    regroup_w(i)
             for a in range(2):
-                if k == 3 + a:
+                if WQ_AT[a] == k:
                     quantise_w(a)
             if live(k - QLAG):
                 quantise_y(k - QLAG)
@@ -210,12 +216,18 @@ def tile_retentivenetwork_pb_kernel(tc, ret, gamma, beta, Wo, bo, out):
             j = k - 1
             if live(j):
                 normalise(j, LOW)
+            if j == 0:
+                nc.scalar.copy(out=gbf[:], in_=gb[:])
+                nc.tensor.transpose(out=gps[:, 0:P], in_=gbf[:], identity=ident[:])
             if live(j - 1):
                 leave_psum(j - 1, HIGH)
                 regroup_y(j - 1, 1)
             if live(j):
                 turn(j, LOW)
                 normalise(j, HIGH)
+            if j == 0:
+                nc.scalar.copy(out=gbT[:], in_=gps[:, 0:16])
+            if live(j):
                 leave_psum(j, LOW)
                 regroup_y(j, 0)
                 turn(j, HIGH)

@@ -22,11 +22,7 @@ GS = 2
 NG = SLOTS // GS
 GT = GS * P
 EPS = 1e-5
-QLAG = 3
-R_ENG = ["S","V"]
-W_ENG = ["V","V","V","V"]
-W_AT = [1,1,2,2]
-WQ_AT = [1,2]
+QLAG = 2
 
 
 def tile_retentivenetwork_pb_kernel(tc, ret, gamma, beta, Wo, bo, out):
@@ -37,10 +33,11 @@ def tile_retentivenetwork_pb_kernel(tc, ret, gamma, beta, Wo, bo, out):
 
     with ExitStack() as ctx:
         const = ctx.enter_context(tc.tile_pool(name="const", bufs=1))
-        small = ctx.enter_context(tc.tile_pool(name="small", bufs=4))
-        zpool = ctx.enter_context(tc.tile_pool(name="zpool", bufs=3))
-        ypool = ctx.enter_context(tc.tile_pool(name="ypool", bufs=4))
-        cpool = ctx.enter_context(tc.tile_pool(name="cpool", bufs=3))
+        small = ctx.enter_context(tc.tile_pool(name="small", bufs=3))
+        zpool = ctx.enter_context(tc.tile_pool(name="zpool", bufs=2))
+        ppool = ctx.enter_context(tc.tile_pool(name="ppool", bufs=2))
+        gpool = ctx.enter_context(tc.tile_pool(name="gpool", bufs=1))
+        cpool = ctx.enter_context(tc.tile_pool(name="cpool", bufs=2))
         opool = ctx.enter_context(tc.tile_pool(name="opool", bufs=3))
         tpsum = ctx.enter_context(tc.psum_pool(name="tpsum", bufs=4))
         apsum = ctx.enter_context(tc.psum_pool(name="apsum", bufs=4))
@@ -65,7 +62,8 @@ def tile_retentivenetwork_pb_kernel(tc, ret, gamma, beta, Wo, bo, out):
         nc.vector.memset(one[:], 1.0)
         nc.scalar.dma_start(out=gb[0:8, :], in_=gamma.rearrange("(h c) -> h c", c=P))
         nc.scalar.dma_start(out=gb[8:16, :], in_=beta.rearrange("(h c) -> h c", c=P))
-        load_x(0)
+        for s in range(GS):
+            nc.sync.dma_start(out=xs[0][:, s, :], in_=ret_v[:, s, :])
         load_x(1)
         load_w(0)
         load_x(2)
@@ -86,18 +84,13 @@ def tile_retentivenetwork_pb_kernel(tc, ret, gamma, beta, Wo, bo, out):
         wc = const.tile([P, 2, E], U32, name="wc", align_bytes=64)
         ws = const.tile([P, 2, E], U8, name="ws", align_bytes=64)
 
-        def regroup(eng, dst, src):
-            if eng == "G":
-                nc.gpsimd.tensor_scalar(out=dst, in0=src.rearrange("p t c -> p c t"), scalar1=1.0, scalar2=0.0, op0=ALU.mult, op1=ALU.add)
-            elif eng == "V":
-                nc.vector.tensor_copy(out=dst.rearrange("p (c i) t -> p c t i", i=4), in_=src.rearrange("p t (c i) -> p c t i", i=4))
-            else:
-                nc.scalar.copy(out=dst.rearrange("p (c i) t -> p c t i", i=4), in_=src.rearrange("p t (c i) -> p c t i", i=4))
-
         def regroup_w(i):
             a, half = divmod(i, 2)
             cols = slice(half * 512, (half + 1) * 512)
-            regroup(W_ENG[i], wgrp[:, a, cols, :], wraw[:, 4 * a:4 * a + 4, cols])
+            nc.vector.tensor_copy(
+                out=wgrp[:, a, cols, :].rearrange("p (c i) t -> p c t i", i=4),
+                in_=wraw[:, 4 * a:4 * a + 4, cols].rearrange("p t (c i) -> p c t i", i=4),
+            )
 
         def quantise_w(a):
             nc.vector.quantize_mx(
@@ -105,18 +98,20 @@ def tile_retentivenetwork_pb_kernel(tc, ret, gamma, beta, Wo, bo, out):
                 in_=wgrp[:, a, :, :].rearrange("p c t -> p (c t)"),
             )
 
-        sums, std, rstd, nb, z, zt, yp, yg, yc, ys, acc = {}, {}, {}, {}, {}, {}, {}, {}, {}, {}, {}
+        st, sums, std, rstd, nb, z, zt, yp, yg, yc, ys, acc, o = {}, {}, {}, {}, {}, {}, {}, {}, {}, {}, {}, {}, {}
         U = GS * H
 
-        def stats_first(g):
-            st = small.tile([P, U, 6], F32, name="st")
+        def measure(g):
+            st[g] = small.tile([P, U, 6], F32, name="st")
             for s in range(GS):
                 for h in range(H):
-                    nc.vector.bn_stats(out=st[:, s * H + h, :], in_=xs[g][:, s, h * P:(h + 1) * P])
+                    nc.vector.bn_stats(out=st[g][:, s * H + h, :], in_=xs[g][:, s, h * P:(h + 1) * P])
+
+        def stats_first(g):
             sums[g] = small.tile([P, U, 3], F32, name="sums")
-            nc.vector.tensor_tensor(out=sums[g][:], in0=st[:, :, 0:3], in1=st[:, :, 3:6], op=ALU.add)
+            nc.vector.tensor_tensor(out=sums[g][:], in0=st[g][:, :, 0:3], in1=st[g][:, :, 3:6], op=ALU.add)
             dif = small.tile([P, U, 1], F32, name="dif")
-            nc.vector.tensor_tensor(out=dif[:], in0=st[:, :, 1:2], in1=st[:, :, 4:5], op=ALU.subtract)
+            nc.vector.tensor_tensor(out=dif[:], in0=st[g][:, :, 1:2], in1=st[g][:, :, 4:5], op=ALU.subtract)
             q32 = small.tile([P, U, 1], F32, name="q32")
             nc.vector.scalar_tensor_tensor(out=q32[:], in0=dif[:], scalar=32.0, in1=dif[:], op0=ALU.mult, op1=ALU.mult)
             w128 = small.tile([P, U, 1], F32, name="w128")
@@ -130,10 +125,9 @@ def tile_retentivenetwork_pb_kernel(tc, ret, gamma, beta, Wo, bo, out):
             nb[g] = small.tile([P, U, 1], F32, name="nb")
             nc.vector.scalar_tensor_tensor(out=nb[g][:], in0=sums[g][:, :, 1:2], scalar=-0.5, in1=rstd[g][:], op0=ALU.mult, op1=ALU.mult)
 
-        def normalise(g, heads):
-            if heads[0] == 0:
-                z[g] = zpool.tile([P, GS, D], F32, name="z")
-            for h in heads:
+        def normalise(g):
+            z[g] = zpool.tile([P, GS, D], F32, name="z")
+            for h in range(H):
                 for s in range(GS):
                     u = s * H + h
                     nc.scalar.activation(
@@ -149,17 +143,20 @@ def tile_retentivenetwork_pb_kernel(tc, ret, gamma, beta, Wo, bo, out):
 
         def leave_psum(g, heads):
             if heads[0] == 0:
-                yp[g] = ypool.tile([P, H, GT], BF16, name="yp")
+                yp[g] = ppool.tile([P, H, GT], BF16, name="yp")
             for h in heads:
                 nc.scalar.activation(
                     out=yp[g][:, h, :], in_=zt[(g, h)][:, 0:GT], func=ACT.Identity,
                     bias=gbT[:, 8 + h:9 + h], scale=gbT[:, h:h + 1],
                 )
 
-        def regroup_y(g, a):
-            if a == 0:
-                yg[g] = ypool.tile([P, 2, GT, 4], BF16, name="yg", align_bytes=64)
-            regroup(R_ENG[a], yg[g][:, a, :, :], yp[g][:, 4 * a:4 * a + 4, :])
+        def regroup_y(g):
+            yg[g] = gpool.tile([P, 2, GT, 4], BF16, name="yg", align_bytes=64)
+            for a in range(2):
+                nc.gpsimd.tensor_scalar(
+                    out=yg[g][:, a, :, :], in0=yp[g][:, 4 * a:4 * a + 4, :].rearrange("p t c -> p c t"),
+                    scalar1=1.0, scalar2=0.0, op0=ALU.mult, op1=ALU.add,
+                )
 
         def quantise_y(g):
             yc[g] = cpool.tile([P, 2 * GT], U32, name="yc", align_bytes=64)
@@ -180,54 +177,52 @@ def tile_retentivenetwork_pb_kernel(tc, ret, gamma, beta, Wo, bo, out):
                             start=(a == 0), stop=(a == 1),
                         )
 
-        def finish(g):
-            o = opool.tile([P, GS, E], F32, name="o")
-            for s in range(GS):
-                for n in range(2):
-                    nc.vector.tensor_tensor(out=o[:, s, n * 512:(n + 1) * 512], in0=acc[(g, s, n)][:], in1=bias_b[:, n * 512:(n + 1) * 512], op=ALU.add)
-
-            nc.sync.dma_start(out=out_v[:, g * GS:(g + 1) * GS, :], in_=o[:])
+        def finish(g, tiles):
+            if tiles[0] == 0:
+                o[g] = opool.tile([P, GS, E], F32, name="o")
+            for i in tiles:
+                s, n = divmod(i, 2)
+                nc.vector.tensor_tensor(out=o[g][:, s, n * 512:(n + 1) * 512], in0=acc[(g, s, n)][:], in1=bias_b[:, n * 512:(n + 1) * 512], op=ALU.add)
+                if n == 1 and g == NG - 1:
+                    nc.sync.dma_start(out=out_v[:, g * GS + s, :], in_=o[g][:, s, :])
+            if tiles[-1] == 3 and g < NG - 1:
+                nc.sync.dma_start(out=out_v[:, g * GS:(g + 1) * GS, :], in_=o[g][:])
 
         def live(g):
             return 0 <= g < NG
 
         LOW = [0, 1, 2, 3]
         HIGH = [4, 5, 6, 7]
-        for i in range(4):
-            if W_ENG[i] == "G":
-                regroup_w(i)
-        for k in range(NG + QLAG + 2):
+        for k in range(NG + QLAG + 1):
+            if live(k):
+                measure(k)
+            if k in (1, 2):
+                regroup_w(2 * k - 2)
+            if live(k - QLAG - 1):
+                finish(k - QLAG - 1, [0, 1, 2])
             if live(k):
                 stats_first(k)
             if live(k - 1):
-                stats_second(k - 1)
-            for i in range(4):
-                if W_ENG[i] != "G" and W_AT[i] == k:
-                    regroup_w(i)
-            for a in range(2):
-                if WQ_AT[a] == k:
-                    quantise_w(a)
+                leave_psum(k - 1, HIGH)
+            if k in (1, 2):
+                regroup_w(2 * k - 1)
+            if live(k - QLAG - 1):
+                finish(k - QLAG - 1, [3])
+            if live(k):
+                stats_second(k)
+            if k in (1, 2):
+                quantise_w(k - 1)
             if live(k - QLAG):
                 quantise_y(k - QLAG)
-            if live(k - QLAG - 1):
-                finish(k - QLAG - 1)
-            if live(k - QLAG):
                 project(k - QLAG)
-            j = k - 1
-            if live(j):
-                normalise(j, LOW)
-            if j == 0:
-                nc.scalar.copy(out=gbf[:], in_=gb[:])
-                nc.tensor.transpose(out=gps[:, 0:P], in_=gbf[:], identity=ident[:])
-            if live(j - 1):
-                leave_psum(j - 1, HIGH)
-                regroup_y(j - 1, 1)
-            if live(j):
-                turn(j, LOW)
-                normalise(j, HIGH)
-            if j == 0:
-                nc.scalar.copy(out=gbT[:], in_=gps[:, 0:16])
-            if live(j):
-                leave_psum(j, LOW)
-                regroup_y(j, 0)
-                turn(j, HIGH)
+            if live(k - 1):
+                regroup_y(k - 1)
+            if live(k):
+                normalise(k)
+                if k == 0:
+                    nc.scalar.copy(out=gbf[:], in_=gb[:])
+                    nc.tensor.transpose(out=gps[:, 0:P], in_=gbf[:], identity=ident[:])
+                    nc.scalar.copy(out=gbT[:], in_=gps[:, 0:16])
+                turn(k, LOW)
+                leave_psum(k, LOW)
+                turn(k, HIGH)

@@ -36,7 +36,7 @@ def tile_retentivenetwork_pb_kernel(tc, ret, gamma, beta, Wo, bo, out):
         small = ctx.enter_context(tc.tile_pool(name="small", bufs=3))
         zpool = ctx.enter_context(tc.tile_pool(name="zpool", bufs=2))
         ppool = ctx.enter_context(tc.tile_pool(name="ppool", bufs=2))
-        gpool = ctx.enter_context(tc.tile_pool(name="gpool", bufs=1))
+        gpool = ctx.enter_context(tc.tile_pool(name="gpool", bufs=2))
         cpool = ctx.enter_context(tc.tile_pool(name="cpool", bufs=2))
         opool = ctx.enter_context(tc.tile_pool(name="opool", bufs=3))
         tpsum = ctx.enter_context(tc.psum_pool(name="tpsum", bufs=4))
@@ -150,12 +150,12 @@ def tile_retentivenetwork_pb_kernel(tc, ret, gamma, beta, Wo, bo, out):
                     bias=gbT[:, 8 + h:9 + h], scale=gbT[:, h:h + 1],
                 )
 
-        def regroup_y(g):
+        def regroup_y(g, go):
             yg[g] = gpool.tile([P, 2, GT, 4], BF16, name="yg", align_bytes=64)
             for a in range(2):
                 nc.gpsimd.tensor_scalar(
                     out=yg[g][:, a, :, :], in0=yp[g][:, 4 * a:4 * a + 4, :].rearrange("p t c -> p c t"),
-                    scalar1=1.0, scalar2=0.0, op0=ALU.mult, op1=ALU.add,
+                    scalar1=go[:, 0:1], scalar2=0.0, op0=ALU.mult, op1=ALU.add,
                 )
 
         def quantise_y(g):
@@ -208,15 +208,17 @@ def tile_retentivenetwork_pb_kernel(tc, ret, gamma, beta, Wo, bo, out):
                 regroup_w(2 * k - 1)
             if live(k - QLAG - 1):
                 finish(k - QLAG - 1, [3])
-            if live(k):
-                stats_second(k)
             if k in (1, 2):
                 quantise_w(k - 1)
             if live(k - QLAG):
                 quantise_y(k - QLAG)
                 project(k - QLAG)
+            if live(k):
+                stats_second(k)
             if live(k - 1):
-                regroup_y(k - 1)
+                go = small.tile([P, 1], F32, name="go")
+                nc.vector.memset(go[:], 1.0)
+                regroup_y(k - 1, go)
             if live(k):
                 normalise(k)
                 if k == 0:

@@ -23,6 +23,7 @@ NG = SLOTS // GS
 GT = GS * P
 EPS = 1e-5
 QLAG = 2
+V_HEADS = [7]
 
 
 def tile_retentivenetwork_pb_kernel(tc, ret, gamma, beta, Wo, bo, out):
@@ -145,10 +146,16 @@ def tile_retentivenetwork_pb_kernel(tc, ret, gamma, beta, Wo, bo, out):
             if heads[0] == 0:
                 yp[g] = ppool.tile([P, H, GT], BF16, name="yp")
             for h in heads:
-                nc.scalar.activation(
-                    out=yp[g][:, h, :], in_=zt[(g, h)][:, 0:GT], func=ACT.Identity,
-                    bias=gbT[:, 8 + h:9 + h], scale=gbT[:, h:h + 1],
-                )
+                if h in V_HEADS:
+                    nc.vector.tensor_scalar(
+                        out=yp[g][:, h, :], in0=zt[(g, h)][:, 0:GT],
+                        scalar1=gbT[:, h:h + 1], scalar2=gbT[:, 8 + h:9 + h], op0=ALU.mult, op1=ALU.add,
+                    )
+                else:
+                    nc.scalar.activation(
+                        out=yp[g][:, h, :], in_=zt[(g, h)][:, 0:GT], func=ACT.Identity,
+                        bias=gbT[:, 8 + h:9 + h], scale=gbT[:, h:h + 1],
+                    )
 
         def regroup_y(g, go):
             yg[g] = gpool.tile([P, 2, GT, 4], BF16, name="yg", align_bytes=64)
@@ -196,6 +203,8 @@ def tile_retentivenetwork_pb_kernel(tc, ret, gamma, beta, Wo, bo, out):
         for k in range(NG + QLAG + 1):
             if live(k):
                 measure(k)
+            if live(k - 1):
+                leave_psum(k - 1, V_HEADS)
             if k in (1, 2):
                 regroup_w(2 * k - 2)
             if live(k - QLAG - 1):
@@ -203,7 +212,7 @@ def tile_retentivenetwork_pb_kernel(tc, ret, gamma, beta, Wo, bo, out):
             if live(k):
                 stats_first(k)
             if live(k - 1):
-                leave_psum(k - 1, HIGH)
+                leave_psum(k - 1, [h for h in HIGH if h not in V_HEADS])
             if k in (1, 2):
                 regroup_w(2 * k - 1)
             if live(k - QLAG - 1):

@@ -23,7 +23,6 @@ NG = SLOTS // GS
 GT = GS * P
 EPS = 1e-5
 QLAG = 2
-V_HEADS = [7]
 
 
 def tile_retentivenetwork_pb_kernel(tc, ret, gamma, beta, Wo, bo, out):
@@ -37,7 +36,7 @@ def tile_retentivenetwork_pb_kernel(tc, ret, gamma, beta, Wo, bo, out):
         small = ctx.enter_context(tc.tile_pool(name="small", bufs=3))
         zpool = ctx.enter_context(tc.tile_pool(name="zpool", bufs=2))
         ppool = ctx.enter_context(tc.tile_pool(name="ppool", bufs=2))
-        gpool = ctx.enter_context(tc.tile_pool(name="gpool", bufs=2))
+        gpool = ctx.enter_context(tc.tile_pool(name="gpool", bufs=1))
         cpool = ctx.enter_context(tc.tile_pool(name="cpool", bufs=2))
         opool = ctx.enter_context(tc.tile_pool(name="opool", bufs=3))
         tpsum = ctx.enter_context(tc.psum_pool(name="tpsum", bufs=4))
@@ -146,24 +145,17 @@ def tile_retentivenetwork_pb_kernel(tc, ret, gamma, beta, Wo, bo, out):
             if heads[0] == 0:
                 yp[g] = ppool.tile([P, H, GT], BF16, name="yp")
             for h in heads:
-                if h in V_HEADS:
-                    nc.vector.tensor_scalar(
-                        out=yp[g][:, h, :], in0=zt[(g, h)][:, 0:GT],
-                        scalar1=gbT[:, h:h + 1], scalar2=gbT[:, 8 + h:9 + h], op0=ALU.mult, op1=ALU.add,
-                    )
-                else:
-                    nc.scalar.activation(
-                        out=yp[g][:, h, :], in_=zt[(g, h)][:, 0:GT], func=ACT.Identity,
-                        bias=gbT[:, 8 + h:9 + h], scale=gbT[:, h:h + 1],
-                    )
-
-        def regroup_y(g, go):
-            yg[g] = gpool.tile([P, 2, GT, 4], BF16, name="yg", align_bytes=64)
-            for a in range(2):
-                nc.gpsimd.tensor_scalar(
-                    out=yg[g][:, a, :, :], in0=yp[g][:, 4 * a:4 * a + 4, :].rearrange("p t c -> p c t"),
-                    scalar1=go[:, 0:1], scalar2=0.0, op0=ALU.mult, op1=ALU.add,
+                nc.scalar.activation(
+                    out=yp[g][:, h, :], in_=zt[(g, h)][:, 0:GT], func=ACT.Identity,
+                    bias=gbT[:, 8 + h:9 + h], scale=gbT[:, h:h + 1],
                 )
+
+        def regroup_y(g):
+            yg[g] = gpool.tile([P, 2, GT, 4], BF16, name="yg", align_bytes=64)
+            nc.gpsimd.tensor_scalar(
+                out=yg[g][:], in0=yp[g][:].rearrange("p (a t) c -> p a c t", a=2),
+                scalar1=1.0, scalar2=0.0, op0=ALU.mult, op1=ALU.add,
+            )
 
         def quantise_y(g):
             yc[g] = cpool.tile([P, 2 * GT], U32, name="yc", align_bytes=64)
@@ -203,8 +195,6 @@ def tile_retentivenetwork_pb_kernel(tc, ret, gamma, beta, Wo, bo, out):
         for k in range(NG + QLAG + 1):
             if live(k):
                 measure(k)
-            if live(k - 1):
-                leave_psum(k - 1, V_HEADS)
             if k in (1, 2):
                 regroup_w(2 * k - 2)
             if live(k - QLAG - 1):
@@ -212,7 +202,7 @@ def tile_retentivenetwork_pb_kernel(tc, ret, gamma, beta, Wo, bo, out):
             if live(k):
                 stats_first(k)
             if live(k - 1):
-                leave_psum(k - 1, [h for h in HIGH if h not in V_HEADS])
+                leave_psum(k - 1, HIGH)
             if k in (1, 2):
                 regroup_w(2 * k - 1)
             if live(k - QLAG - 1):
@@ -225,9 +215,7 @@ def tile_retentivenetwork_pb_kernel(tc, ret, gamma, beta, Wo, bo, out):
             if live(k):
                 stats_second(k)
             if live(k - 1):
-                go = small.tile([P, 1], F32, name="go")
-                nc.vector.memset(go[:], 1.0)
-                regroup_y(k - 1, go)
+                regroup_y(k - 1)
             if live(k):
                 normalise(k)
                 if k == 0:

@@ -17,12 +17,18 @@ P = 128
 D = 1024
 E = 1024
 H = 8
+PASSES = 2
+PACK = 4
+BANK = 512
 SLOTS = 16
 GS = 2
 NG = SLOTS // GS
 GT = GS * P
+U = GS * H
 EPS = 1e-5
 QLAG = 2
+LOW = [0, 1, 2, 3]
+HIGH = [4, 5, 6, 7]
 
 
 def tile_retentivenetwork_pb_kernel(tc, ret, gamma, beta, Wo, bo, out):
@@ -36,7 +42,7 @@ def tile_retentivenetwork_pb_kernel(tc, ret, gamma, beta, Wo, bo, out):
         small = ctx.enter_context(tc.tile_pool(name="small", bufs=3))
         zpool = ctx.enter_context(tc.tile_pool(name="zpool", bufs=2))
         ppool = ctx.enter_context(tc.tile_pool(name="ppool", bufs=2))
-        gpool = ctx.enter_context(tc.tile_pool(name="gpool", bufs=1))
+        gpool = ctx.enter_context(tc.tile_pool(name="gpool", bufs=2))
         cpool = ctx.enter_context(tc.tile_pool(name="cpool", bufs=2))
         opool = ctx.enter_context(tc.tile_pool(name="opool", bufs=3))
         tpsum = ctx.enter_context(tc.psum_pool(name="tpsum", bufs=4))
@@ -47,21 +53,21 @@ def tile_retentivenetwork_pb_kernel(tc, ret, gamma, beta, Wo, bo, out):
         for g in range(NG):
             xg = const.tile([P, GS, D], BF16, name="x%d" % g)
             xs.append(xg)
-        wraw = const.tile([P, 8, E], BF16, name="wraw")
+        wraw = const.tile([P, PASSES * PACK, E], BF16, name="wraw")
         bias_b = const.tile([P, E], BF16, name="bias_b")
 
         def load_x(g):
             nc.sync.dma_start(out=xs[g][:], in_=ret_v[:, g * GS:(g + 1) * GS, :])
 
         def load_w(a):
-            nc.sync.dma_start(out=wraw[:, 4 * a:4 * a + 4, :], in_=wo_v[:, 4 * a:4 * a + 4, :])
+            nc.sync.dma_start(out=wraw[:, PACK * a:PACK * (a + 1), :], in_=wo_v[:, PACK * a:PACK * (a + 1), :])
 
         gb = const.tile([P, P], BF16, name="gb")
         nc.vector.memset(gb[:], 0.0)
         one = const.tile([P, 1], F32, name="one")
         nc.vector.memset(one[:], 1.0)
-        nc.scalar.dma_start(out=gb[0:8, :], in_=gamma.rearrange("(h c) -> h c", c=P))
-        nc.scalar.dma_start(out=gb[8:16, :], in_=beta.rearrange("(h c) -> h c", c=P))
+        nc.scalar.dma_start(out=gb[0:H, :], in_=gamma.rearrange("(h c) -> h c", c=P))
+        nc.scalar.dma_start(out=gb[H:2 * H, :], in_=beta.rearrange("(h c) -> h c", c=P))
         for s in range(GS):
             nc.sync.dma_start(out=xs[0][:, s, :], in_=ret_v[:, s, :])
         load_x(1)
@@ -72,24 +78,29 @@ def tile_retentivenetwork_pb_kernel(tc, ret, gamma, beta, Wo, bo, out):
             load_x(g)
         nc.sync.dma_start(out=bias_b[:], in_=bo.partition_broadcast(P))
         warm = const.tile([P, 1], F32, name="warm")
-        nc.scalar.activation(out=warm[:], in_=one[:], func=ACT.Sqrt)
+        nc.scalar.activation(out=warm[:], in_=one[:], func=ACT.Abs_reciprocal_sqrt)
 
         ident = const.tile([P, P], F32, name="ident")
         make_identity(nc, ident[:])
         gbf = const.tile([P, P], F32, name="gbf")
-        gbT = const.tile([P, 16], F32, name="gbT")
-        gps = apsum.tile([P, 512], F32, tag="acc", name="gps")
+        gbT = const.tile([P, 2 * H], F32, name="gbT")
+        gps = apsum.tile([P, BANK], F32, tag="acc", name="gps")
 
-        wgrp = const.tile([P, 2, E, 4], BF16, name="wgrp", align_bytes=64)
-        wc = const.tile([P, 2, E], U32, name="wc", align_bytes=64)
-        ws = const.tile([P, 2, E], U8, name="ws", align_bytes=64)
+        def turn_gamma_beta():
+            nc.scalar.copy(out=gbf[:], in_=gb[:])
+            nc.tensor.transpose(out=gps[:, 0:P], in_=gbf[:], identity=ident[:])
+            nc.scalar.copy(out=gbT[:], in_=gps[:, 0:2 * H])
+
+        wgrp = const.tile([P, PASSES, E, PACK], BF16, name="wgrp", align_bytes=64)
+        wc = const.tile([P, PASSES, E], U32, name="wc", align_bytes=64)
+        ws = const.tile([P, PASSES, E], U8, name="ws", align_bytes=64)
 
         def regroup_w(i):
             a, half = divmod(i, 2)
-            cols = slice(half * 512, (half + 1) * 512)
+            cols = slice(half * BANK, (half + 1) * BANK)
             nc.vector.tensor_copy(
                 out=wgrp[:, a, cols, :].rearrange("p (c i) t -> p c t i", i=4),
-                in_=wraw[:, 4 * a:4 * a + 4, cols].rearrange("p t (c i) -> p c t i", i=4),
+                in_=wraw[:, PACK * a:PACK * (a + 1), cols].rearrange("p t (c i) -> p c t i", i=4),
             )
 
         def quantise_w(a):
@@ -98,8 +109,7 @@ def tile_retentivenetwork_pb_kernel(tc, ret, gamma, beta, Wo, bo, out):
                 in_=wgrp[:, a, :, :].rearrange("p c t -> p (c t)"),
             )
 
-        st, sums, std, rstd, nb, z, zt, yp, yg, yc, ys, acc, o = {}, {}, {}, {}, {}, {}, {}, {}, {}, {}, {}, {}, {}
-        U = GS * H
+        st, sums, rstd, nb, z, zt, yp, yg, yc, ys, acc, o = {}, {}, {}, {}, {}, {}, {}, {}, {}, {}, {}, {}
 
         def measure(g):
             st[g] = small.tile([P, U, 6], F32, name="st")
@@ -116,12 +126,10 @@ def tile_retentivenetwork_pb_kernel(tc, ret, gamma, beta, Wo, bo, out):
             nc.vector.scalar_tensor_tensor(out=q32[:], in0=dif[:], scalar=32.0, in1=dif[:], op0=ALU.mult, op1=ALU.mult)
             w128 = small.tile([P, U, 1], F32, name="w128")
             nc.vector.scalar_tensor_tensor(out=w128[:], in0=q32[:], scalar=P * EPS, in1=sums[g][:, :, 2:3], op0=ALU.add, op1=ALU.add)
-            std[g] = small.tile([P, U, 1], F32, name="std")
-            nc.scalar.activation(out=std[g][:], in_=w128[:], func=ACT.Sqrt, scale=1.0 / P)
+            rstd[g] = small.tile([P, U, 1], F32, name="rstd")
+            nc.scalar.activation(out=rstd[g][:], in_=w128[:], func=ACT.Abs_reciprocal_sqrt, scale=1.0 / P)
 
         def stats_second(g):
-            rstd[g] = small.tile([P, U, 1], F32, name="rstd")
-            nc.vector.reciprocal(out=rstd[g][:], in_=std[g][:])
             nb[g] = small.tile([P, U, 1], F32, name="nb")
             nc.vector.scalar_tensor_tensor(out=nb[g][:], in0=sums[g][:, :, 1:2], scalar=-0.5, in1=rstd[g][:], op0=ALU.mult, op1=ALU.mult)
 
@@ -137,7 +145,7 @@ def tile_retentivenetwork_pb_kernel(tc, ret, gamma, beta, Wo, bo, out):
 
         def turn(g, heads):
             for h in heads:
-                zt[(g, h)] = tpsum.tile([P, 512], F32, tag="zt", name="zt")
+                zt[(g, h)] = tpsum.tile([P, BANK], F32, tag="zt", name="zt")
                 for s in range(GS):
                     nc.tensor.transpose(out=zt[(g, h)][:, s * P:(s + 1) * P], in_=z[g][:, s, h * P:(h + 1) * P], identity=ident[:])
 
@@ -147,51 +155,50 @@ def tile_retentivenetwork_pb_kernel(tc, ret, gamma, beta, Wo, bo, out):
             for h in heads:
                 nc.scalar.activation(
                     out=yp[g][:, h, :], in_=zt[(g, h)][:, 0:GT], func=ACT.Identity,
-                    bias=gbT[:, 8 + h:9 + h], scale=gbT[:, h:h + 1],
+                    bias=gbT[:, H + h:H + h + 1], scale=gbT[:, h:h + 1],
                 )
 
-        def regroup_y(g):
-            yg[g] = gpool.tile([P, 2, GT, 4], BF16, name="yg", align_bytes=64)
-            nc.gpsimd.tensor_scalar(
-                out=yg[g][:], in0=yp[g][:].rearrange("p (a t) c -> p a c t", a=2),
-                scalar1=1.0, scalar2=0.0, op0=ALU.mult, op1=ALU.add,
-            )
+        def regroup_y(g, go):
+            yg[g] = gpool.tile([P, PASSES, GT, PACK], BF16, name="yg", align_bytes=64)
+            for a in range(PASSES):
+                nc.gpsimd.tensor_scalar(
+                    out=yg[g][:, a, :, :], in0=yp[g][:, PACK * a:PACK * (a + 1), :].rearrange("p t c -> p c t"),
+                    scalar1=go[:, 0:1], scalar2=0.0, op0=ALU.mult, op1=ALU.add,
+                )
 
         def quantise_y(g):
-            yc[g] = cpool.tile([P, 2 * GT], U32, name="yc", align_bytes=64)
-            ys[g] = cpool.tile([P, 2 * GT], U8, name="ys", align_bytes=64)
+            yc[g] = cpool.tile([P, PASSES * GT], U32, name="yc", align_bytes=64)
+            ys[g] = cpool.tile([P, PASSES * GT], U8, name="ys", align_bytes=64)
             nc.vector.quantize_mx(out=yc[g][:].bitcast(FP8X4), scales=ys[g][:], in_=yg[g][:].rearrange("p a c t -> p (a c t)"))
 
         def project(g):
             for s in range(GS):
-                for n in range(2):
-                    acc[(g, s, n)] = apsum.tile([P, 512], F32, tag="acc", name="acc")
-                    for a in range(2):
+                for n in range(E // BANK):
+                    acc[(g, s, n)] = apsum.tile([P, BANK], F32, tag="acc", name="acc")
+                    for a in range(PASSES):
                         m_cols = slice(a * GT + s * P, a * GT + (s + 1) * P)
-                        n_cols = slice(n * 512, (n + 1) * 512)
+                        n_cols = slice(n * BANK, (n + 1) * BANK)
                         nc.tensor.matmul_mx(
                             out=acc[(g, s, n)][:],
                             lhsT=yc[g][:, m_cols].bitcast(FP8X4), lhsT_scale=ys[g][:, m_cols],
                             rhs=wc[:, a, n_cols].bitcast(FP8X4), rhs_scale=ws[:, a, n_cols],
-                            start=(a == 0), stop=(a == 1),
+                            start=(a == 0), stop=(a == PASSES - 1),
                         )
 
-        def finish(g, tiles):
-            if tiles[0] == 0:
+        def finish(g, banks):
+            if banks[0] == 0:
                 o[g] = opool.tile([P, GS, E], F32, name="o")
-            for i in tiles:
+            for i in banks:
                 s, n = divmod(i, 2)
-                nc.vector.tensor_tensor(out=o[g][:, s, n * 512:(n + 1) * 512], in0=acc[(g, s, n)][:], in1=bias_b[:, n * 512:(n + 1) * 512], op=ALU.add)
+                nc.vector.tensor_tensor(out=o[g][:, s, n * BANK:(n + 1) * BANK], in0=acc[(g, s, n)][:], in1=bias_b[:, n * BANK:(n + 1) * BANK], op=ALU.add)
                 if n == 1 and g == NG - 1:
                     nc.sync.dma_start(out=out_v[:, g * GS + s, :], in_=o[g][:, s, :])
-            if tiles[-1] == 3 and g < NG - 1:
+            if banks[-1] == 3 and g < NG - 1:
                 nc.sync.dma_start(out=out_v[:, g * GS:(g + 1) * GS, :], in_=o[g][:])
 
         def live(g):
             return 0 <= g < NG
 
-        LOW = [0, 1, 2, 3]
-        HIGH = [4, 5, 6, 7]
         for k in range(NG + QLAG + 1):
             if live(k):
                 measure(k)
@@ -215,13 +222,13 @@ def tile_retentivenetwork_pb_kernel(tc, ret, gamma, beta, Wo, bo, out):
             if live(k):
                 stats_second(k)
             if live(k - 1):
-                regroup_y(k - 1)
+                go = small.tile([P, 1], F32, name="go")
+                nc.vector.memset(go[:], 1.0)
+                regroup_y(k - 1, go)
             if live(k):
                 normalise(k)
                 if k == 0:
-                    nc.scalar.copy(out=gbf[:], in_=gb[:])
-                    nc.tensor.transpose(out=gps[:, 0:P], in_=gbf[:], identity=ident[:])
-                    nc.scalar.copy(out=gbT[:], in_=gps[:, 0:16])
+                    turn_gamma_beta()
                 turn(k, LOW)
                 leave_psum(k, LOW)
                 turn(k, HIGH)

from contextlib import ExitStack

import concourse.mybir as mybir
from concourse.masks import make_identity

FLOPS = 2 * 2048 * 1024 * 1024

BF16 = mybir.dt.bfloat16
F32 = mybir.dt.float32
U32 = mybir.dt.uint32
U8 = mybir.dt.uint8
FP8X4 = mybir.dt.float8_e4m3fn_x4
ALU = mybir.AluOpType
ACT = mybir.ActivationFunctionType

P = 128
D = 1024
E = 1024
H = 8
PASSES = 2
PACK = 4
BANK = 512
SLOTS = 16
GS = 2
NG = SLOTS // GS
GT = GS * P
U = GS * H
EPS = 1e-5
QLAG = 2
LOW = [0, 1, 2, 3]
HIGH = [4, 5, 6, 7]


def tile_retentivenetwork_pb_kernel(tc, ret, gamma, beta, Wo, bo, out):
    nc = tc.nc
    ret_v = ret.rearrange("b (q j) h c -> (b q) j (h c)", j=SLOTS)
    out_v = out.rearrange("b (q j) e -> (b q) j e", j=SLOTS)
    wo_v = Wo.rearrange("(a p) n -> p a n", p=P)

    with ExitStack() as ctx:
        const = ctx.enter_context(tc.tile_pool(name="const", bufs=1))
        small = ctx.enter_context(tc.tile_pool(name="small", bufs=3))
        zpool = ctx.enter_context(tc.tile_pool(name="zpool", bufs=2))
        ppool = ctx.enter_context(tc.tile_pool(name="ppool", bufs=2))
        gpool = ctx.enter_context(tc.tile_pool(name="gpool", bufs=2))
        cpool = ctx.enter_context(tc.tile_pool(name="cpool", bufs=2))
        opool = ctx.enter_context(tc.tile_pool(name="opool", bufs=3))
        tpsum = ctx.enter_context(tc.psum_pool(name="tpsum", bufs=4))
        apsum = ctx.enter_context(tc.psum_pool(name="apsum", bufs=4))
        ctx.enter_context(tc.manual_schedule())

        xs = []
        for g in range(NG):
            xg = const.tile([P, GS, D], BF16, name="x%d" % g)
            xs.append(xg)
        wraw = const.tile([P, PASSES * PACK, E], BF16, name="wraw")
        bias_b = const.tile([P, E], BF16, name="bias_b")

        def load_x(g):
            nc.sync.dma_start(out=xs[g][:], in_=ret_v[:, g * GS:(g + 1) * GS, :])

        def load_w(a):
            nc.sync.dma_start(out=wraw[:, PACK * a:PACK * (a + 1), :], in_=wo_v[:, PACK * a:PACK * (a + 1), :])

        gb = const.tile([P, P], BF16, name="gb")
        nc.vector.memset(gb[:], 0.0)
        one = const.tile([P, 1], F32, name="one")
        nc.vector.memset(one[:], 1.0)
        nc.scalar.dma_start(out=gb[0:H, :], in_=gamma.rearrange("(h c) -> h c", c=P))
        nc.scalar.dma_start(out=gb[H:2 * H, :], in_=beta.rearrange("(h c) -> h c", c=P))
        for s in range(GS):
            nc.sync.dma_start(out=xs[0][:, s, :], in_=ret_v[:, s, :])
        load_x(1)
        load_w(0)
        load_x(2)
        load_w(1)
        for g in range(3, NG):
            load_x(g)
        nc.sync.dma_start(out=bias_b[:], in_=bo.partition_broadcast(P))
        warm = const.tile([P, 1], F32, name="warm")
        nc.scalar.activation(out=warm[:], in_=one[:], func=ACT.Abs_reciprocal_sqrt)

        ident = const.tile([P, P], F32, name="ident")
        make_identity(nc, ident[:])
        gbf = const.tile([P, P], F32, name="gbf")
        gbT = const.tile([P, 2 * H], F32, name="gbT")
        gps = apsum.tile([P, BANK], F32, tag="acc", name="gps")

        def turn_gamma_beta():
            nc.scalar.copy(out=gbf[:], in_=gb[:])
            nc.tensor.transpose(out=gps[:, 0:P], in_=gbf[:], identity=ident[:])
            nc.scalar.copy(out=gbT[:], in_=gps[:, 0:2 * H])

        wgrp = const.tile([P, PASSES, E, PACK], BF16, name="wgrp", align_bytes=64)
        wc = const.tile([P, PASSES, E], U32, name="wc", align_bytes=64)
        ws = const.tile([P, PASSES, E], U8, name="ws", align_bytes=64)

        def regroup_w(i):
            a, half = divmod(i, 2)
            cols = slice(half * BANK, (half + 1) * BANK)
            nc.vector.tensor_copy(
                out=wgrp[:, a, cols, :].rearrange("p (c i) t -> p c t i", i=4),
                in_=wraw[:, PACK * a:PACK * (a + 1), cols].rearrange("p t (c i) -> p c t i", i=4),
            )

        def quantise_w(a):
            nc.vector.quantize_mx(
                out=wc[:, a, :].bitcast(FP8X4), scales=ws[:, a, :],
                in_=wgrp[:, a, :, :].rearrange("p c t -> p (c t)"),
            )

        st, sums, rstd, nb, z, zt, yp, yg, yc, ys, acc, o = {}, {}, {}, {}, {}, {}, {}, {}, {}, {}, {}, {}

        def measure(g):
            st[g] = small.tile([P, U, 6], F32, name="st")
            for s in range(GS):
                for h in range(H):
                    nc.vector.bn_stats(out=st[g][:, s * H + h, :], in_=xs[g][:, s, h * P:(h + 1) * P])

        def stats_first(g):
            sums[g] = small.tile([P, U, 3], F32, name="sums")
            nc.vector.tensor_tensor(out=sums[g][:], in0=st[g][:, :, 0:3], in1=st[g][:, :, 3:6], op=ALU.add)
            dif = small.tile([P, U, 1], F32, name="dif")
            nc.vector.tensor_tensor(out=dif[:], in0=st[g][:, :, 1:2], in1=st[g][:, :, 4:5], op=ALU.subtract)
            q32 = small.tile([P, U, 1], F32, name="q32")
            nc.vector.scalar_tensor_tensor(out=q32[:], in0=dif[:], scalar=32.0, in1=dif[:], op0=ALU.mult, op1=ALU.mult)
            w128 = small.tile([P, U, 1], F32, name="w128")
            nc.vector.scalar_tensor_tensor(out=w128[:], in0=q32[:], scalar=P * EPS, in1=sums[g][:, :, 2:3], op0=ALU.add, op1=ALU.add)
            rstd[g] = small.tile([P, U, 1], F32, name="rstd")
            nc.scalar.activation(out=rstd[g][:], in_=w128[:], func=ACT.Abs_reciprocal_sqrt, scale=1.0 / P)

        def stats_second(g):
            nb[g] = small.tile([P, U, 1], F32, name="nb")
            nc.vector.scalar_tensor_tensor(out=nb[g][:], in0=sums[g][:, :, 1:2], scalar=-0.5, in1=rstd[g][:], op0=ALU.mult, op1=ALU.mult)

        def normalise(g):
            z[g] = zpool.tile([P, GS, D], F32, name="z")
            for h in range(H):
                for s in range(GS):
                    u = s * H + h
                    nc.scalar.activation(
                        out=z[g][:, s, h * P:(h + 1) * P], in_=xs[g][:, s, h * P:(h + 1) * P],
                        func=ACT.Identity, bias=nb[g][:, u, :], scale=rstd[g][:, u, :],
                    )

        def turn(g, heads):
            for h in heads:
                zt[(g, h)] = tpsum.tile([P, BANK], F32, tag="zt", name="zt")
                for s in range(GS):
                    nc.tensor.transpose(out=zt[(g, h)][:, s * P:(s + 1) * P], in_=z[g][:, s, h * P:(h + 1) * P], identity=ident[:])

        def leave_psum(g, heads):
            if heads[0] == 0:
                yp[g] = ppool.tile([P, H, GT], BF16, name="yp")
            for h in heads:
                nc.scalar.activation(
                    out=yp[g][:, h, :], in_=zt[(g, h)][:, 0:GT], func=ACT.Identity,
                    bias=gbT[:, H + h:H + h + 1], scale=gbT[:, h:h + 1],
                )

        def regroup_y(g, go):
            yg[g] = gpool.tile([P, PASSES, GT, PACK], BF16, name="yg", align_bytes=64)
            for a in range(PASSES):
                nc.gpsimd.tensor_scalar(
                    out=yg[g][:, a, :, :], in0=yp[g][:, PACK * a:PACK * (a + 1), :].rearrange("p t c -> p c t"),
                    scalar1=go[:, 0:1], scalar2=0.0, op0=ALU.mult, op1=ALU.add,
                )

        def quantise_y(g):
            yc[g] = cpool.tile([P, PASSES * GT], U32, name="yc", align_bytes=64)
            ys[g] = cpool.tile([P, PASSES * GT], U8, name="ys", align_bytes=64)
            nc.vector.quantize_mx(out=yc[g][:].bitcast(FP8X4), scales=ys[g][:], in_=yg[g][:].rearrange("p a c t -> p (a c t)"))

        def project(g):
            for s in range(GS):
                for n in range(E // BANK):
                    acc[(g, s, n)] = apsum.tile([P, BANK], F32, tag="acc", name="acc")
                    for a in range(PASSES):
                        m_cols = slice(a * GT + s * P, a * GT + (s + 1) * P)
                        n_cols = slice(n * BANK, (n + 1) * BANK)
                        nc.tensor.matmul_mx(
                            out=acc[(g, s, n)][:],
                            lhsT=yc[g][:, m_cols].bitcast(FP8X4), lhsT_scale=ys[g][:, m_cols],
                            rhs=wc[:, a, n_cols].bitcast(FP8X4), rhs_scale=ws[:, a, n_cols],
                            start=(a == 0), stop=(a == PASSES - 1),
                        )

        def finish(g, banks):
            if banks[0] == 0:
                o[g] = opool.tile([P, GS, E], F32, name="o")
            for i in banks:
                s, n = divmod(i, 2)
                nc.vector.tensor_tensor(out=o[g][:, s, n * BANK:(n + 1) * BANK], in0=acc[(g, s, n)][:], in1=bias_b[:, n * BANK:(n + 1) * BANK], op=ALU.add)
                if n == 1 and g == NG - 1:
                    nc.sync.dma_start(out=out_v[:, g * GS + s, :], in_=o[g][:, s, :])
            if banks[-1] == 3 and g < NG - 1:
                nc.sync.dma_start(out=out_v[:, g * GS:(g + 1) * GS, :], in_=o[g][:])

        def live(g):
            return 0 <= g < NG

        for k in range(NG + QLAG + 1):
            if live(k):
                measure(k)
            if k in (1, 2):
                regroup_w(2 * k - 2)
            if live(k - QLAG - 1):
                finish(k - QLAG - 1, [0, 1, 2])
            if live(k):
                stats_first(k)
            if live(k - 1):
                leave_psum(k - 1, HIGH)
            if k in (1, 2):
                regroup_w(2 * k - 1)
            if live(k - QLAG - 1):
                finish(k - QLAG - 1, [3])
            if k in (1, 2):
                quantise_w(k - 1)
            if live(k - QLAG):
                quantise_y(k - QLAG)
                project(k - QLAG)
            if live(k):
                stats_second(k)
            if live(k - 1):
                go = small.tile([P, 1], F32, name="go")
                nc.vector.memset(go[:], 1.0)
                regroup_y(k - 1, go)
            if live(k):
                normalise(k)
                if k == 0:
                    turn_gamma_beta()
                turn(k, LOW)
                leave_psum(k, LOW)
                turn(k, HIGH)
